import numpy as np
import ml_dtypes


def mxq(x, axis, fmt="e4m3"):
    dtype, down = {"e4m3": (ml_dtypes.float8_e4m3fn, 7), "e5m2": (ml_dtypes.float8_e5m2, 14)}[fmt]
    v = np.moveaxis(np.asarray(x, np.float32).astype(ml_dtypes.bfloat16).astype(np.float64), axis, -1)
    blocks = v.reshape(v.shape[:-1] + (-1, 32))
    amax = np.abs(blocks).max(-1, keepdims=True)
    byte = np.maximum(np.where(amax > 0, np.frexp(amax)[1] - 1 + 127, 0) - down, 1)
    scale = np.exp2(byte - 127.0)
    codes = (blocks / scale).astype(np.float32).astype(dtype).astype(np.float64)
    return np.moveaxis((codes * scale).reshape(v.shape), -1, axis)


WIDE = False


def mx_kscale(k):
    if not WIDE:
        return np.ones(k)
    levels = np.array([20, -20, 10, -10, 0])
    a = np.random.permutation(np.resize(levels, k // 512 * 4)).reshape(k // 512, 4)
    idx = np.arange(k)
    return np.exp2(a[idx // 512, idx % 128 // 32])


BF16 = ml_dtypes.bfloat16


def bf(x):
    return np.asarray(x, np.float32).astype(BF16)


def f64(x):
    return np.asarray(x).astype(np.float64)


B, HH, WW, C, NH, KD, WS, SS = 1, 32, 32, 512, 8, 32, 8, 4
GH, GW, T, F = HH // WS, WW // WS, WS * WS, NH * KD
N = B * GH * GW


def setup_inputs():
    u = mx_kscale(C)
    attn_ctx = np.random.standard_normal((N, T, NH, KD)) * 0.4
    x = np.random.standard_normal((B, HH, WW, C))
    wo = np.random.standard_normal((NH, KD, C)) * 2.0 / np.sqrt(F) / u
    bo = np.random.standard_normal(C) * 0.3
    g = np.random.standard_normal((B, HH, WW, C)) * np.exp2(np.random.randint(-12, 1, (B, HH, WW, 1))) * 4.0 * u
    return {"attn_ctx": bf(attn_ctx), "x": bf(x), "wo": bf(wo), "bo": bf(bo), "grad_out": bf(g)}


def reference(attn_ctx, x, wo, bo, grad_out):
    g = np.roll(f64(grad_out), shift=(-SS, -SS), axis=(1, 2))
    g = g.reshape(B, GH, WS, GW, WS, C).swapaxes(2, 3).reshape(N * T, C)
    go = mxq(g, 1, "e5m2") @ mxq(f64(wo).reshape(F, C), 1, "e4m3").T
    return go.reshape(N, T, NH, KD)

@@ -1,0 +1,165 @@
+from contextlib import ExitStack
+
+import concourse.mybir as mybir
+from concourse.masks import make_identity
+
+BF16 = mybir.dt.bfloat16
+F32 = mybir.dt.float32
+I32 = mybir.dt.int32
+U32 = mybir.dt.uint32
+U8 = mybir.dt.uint8
+E5M2_X4 = mybir.dt.float8_e5m2_x4
+E4M3_X4 = mybir.dt.float8_e4m3fn_x4
+
+P = 128
+HEIGHT = 32
+WIDTH = 32
+CHANNELS = 512
+FEATURES = 256
+WINDOW = 8
+SHIFT = 4
+BANDS = HEIGHT // WINDOW
+WINDOWS_IN_BAND = WIDTH // WINDOW
+PAIR = 2
+PAIRS_IN_ROW = WIDTH // PAIR
+PAIRS_IN_WINDOW_ROW = WINDOW // PAIR
+HALVES = 2
+PACK = 4
+MOVING_COLUMNS = 512
+
+FLOPS = 2 * HEIGHT * WIDTH * FEATURES * CHANNELS
+BYTES = 2 * HEIGHT * WIDTH * CHANNELS + 2 * FEATURES * CHANNELS + 4 * HEIGHT * WIDTH * FEATURES
+
+
+def make_window_order(nc, window_order, identity):
+    moved = SHIFT // PAIR
+    from_image = identity.rearrange("p (row pair) -> p row pair", pair=PAIRS_IN_ROW)
+    to_window = window_order.rearrange(
+        "p (win row pair) -> p win row pair", win=WINDOWS_IN_BAND, row=WINDOW
+    )
+    last = WINDOWS_IN_BAND - 1
+    kept = PAIRS_IN_WINDOW_ROW - moved
+    nc.vector.tensor_copy(
+        out=to_window[:, 0:last],
+        in_=from_image[:, :, moved : moved + last * PAIRS_IN_WINDOW_ROW].rearrange(
+            "p row (win pair) -> p win row pair", pair=PAIRS_IN_WINDOW_ROW
+        ),
+    )
+    nc.vector.tensor_copy(
+        out=to_window[:, last, :, 0:kept], in_=from_image[:, :, PAIRS_IN_ROW - kept : PAIRS_IN_ROW]
+    )
+    nc.vector.tensor_copy(
+        out=to_window[:, last, :, kept:PAIRS_IN_WINDOW_ROW], in_=from_image[:, :, 0:moved]
+    )
+
+
+def transpose_rows(nc, bank, rows, column_order):
+    words = rows.bitcast(F32)
+    for half in range(HALVES):
+        nc.tensor.transpose(
+            out=bank[:, half, :], in_=words[:, half * P : (half + 1) * P], identity=column_order
+        )
+
+
+def regroup(copy, grouped, bank):
+    copy(
+        out=grouped.bitcast(F32).rearrange("p (j half) -> p j half", half=HALVES),
+        in_=bank[:].rearrange("p half j -> p j half"),
+    )
+
+
+def tile_windowattentionblock_pb_s_kernel(tc, attn_ctx, x, wo, bo, grad_out, out):
+    nc = tc.nc
+    image = grad_out.rearrange("b i j c -> (b i j) c")
+    wo_rows = wo.rearrange("h d c -> (h d) c")
+    out_rows = out.rearrange("n t h d -> (n t) (h d)")
+
+    with ExitStack() as pools:
+        keep = pools.enter_context(tc.tile_pool(name="keep", bufs=1))
+        bands = pools.enter_context(tc.tile_pool(name="bands", bufs=BANDS))
+        psum = pools.enter_context(tc.psum_pool(name="psum", bufs=2))
+
+        wo_sb = keep.tile([P, PAIR, CHANNELS], BF16)
+        nc.sync.dma_start(out=wo_sb[:], in_=wo_rows.rearrange("(a p) c -> p a c", p=P))
+        band_pixels = []
+        for band in range(BANDS):
+            pixels = bands.tile([P, PAIR, CHANNELS], BF16, name="pixels")
+            first_row = WINDOW * band + SHIFT
+            rows_above_edge = min(WINDOW, HEIGHT - first_row)
+            split = rows_above_edge * PAIRS_IN_ROW
+            nc.sync.dma_start(
+                out=pixels[0:split],
+                in_=image[first_row * WIDTH : (first_row + rows_above_edge) * WIDTH].rearrange(
+                    "(p e) c -> p e c", e=PAIR
+                ),
+            )
+            if split < P:
+                nc.sync.dma_start(
+                    out=pixels[split:P],
+                    in_=image[0 : (WINDOW - rows_above_edge) * WIDTH].rearrange(
+                        "(p e) c -> p e c", e=PAIR
+                    ),
+                )
+            band_pixels.append(pixels)
+
+        identity = keep.tile([P, P], F32)
+        make_identity(nc, identity[:])
+        window_order = keep.tile([P, P], F32)
+        make_window_order(nc, window_order[:], identity[:])
+
+        wo_codes = keep.tile([P, MOVING_COLUMNS], U32, align_bytes=64)
+        wo_scales = keep.tile([P, MOVING_COLUMNS], U8, align_bytes=64)
+        nc.vector.memset(wo_codes[:, FEATURES:MOVING_COLUMNS].bitcast(I32), 0)
+        nc.vector.memset(wo_scales[:, FEATURES:MOVING_COLUMNS].bitcast(I32), 0)
+
+        def quantise(rows_sb, column_order, codes, scales, fp8_x4):
+            grouped = bands.tile([P, PAIR, P * PACK], BF16, align_bytes=64, name="grouped")
+            even_bank = psum.tile([P, HALVES, P], F32, name="even_bank")
+            odd_bank = psum.tile([P, HALVES, P], F32, name="odd_bank")
+            transpose_rows(nc, even_bank, rows_sb[:, 0, :], column_order)
+            transpose_rows(nc, odd_bank, rows_sb[:, 1, :], column_order)
+            regroup(nc.vector.tensor_copy, grouped[:, 0, :], even_bank)
+            regroup(nc.scalar.copy, grouped[:, 1, :], odd_bank)
+            nc.vector.quantize_mx(
+                out=codes.bitcast(fp8_x4),
+                scales=scales,
+                in_=grouped[:].rearrange("p e v -> p (e v)"),
+            )
+
+        def prepare(band):
+            codes = bands.tile([P, PAIR * P], U32, align_bytes=64, name="codes")
+            scales = bands.tile([P, PAIR * P], U8, align_bytes=64, name="scales")
+            quantise(band_pixels[band], window_order[:], codes[:], scales[:], E5M2_X4)
+            return codes, scales
+
+        def multiply_and_store(band, codes, scales):
+            result = bands.tile([P, PAIR, FEATURES], F32, name="result")
+            even_sums = psum.tile([P, MOVING_COLUMNS], F32, name="even_sums")
+            odd_sums = psum.tile([P, MOVING_COLUMNS], F32, name="odd_sums")
+            for e, sums in enumerate((even_sums, odd_sums)):
+                nc.tensor.matmul_mx(
+                    out=sums[:],
+                    lhsT=codes[:, e * P : (e + 1) * P].bitcast(E5M2_X4),
+                    lhsT_scale=scales[:, e * P : (e + 1) * P],
+                    rhs=wo_codes[:].bitcast(E4M3_X4),
+                    rhs_scale=wo_scales[:],
+                    start=True,
+                    stop=True,
+                )
+            nc.vector.tensor_copy(out=result[:, 0, :], in_=even_sums[:, 0:FEATURES])
+            nc.scalar.copy(out=result[:, 1, :], in_=odd_sums[:, 0:FEATURES])
+            nc.sync.dma_start(
+                out=out_rows[band * PAIR * P : (band + 1) * PAIR * P].rearrange(
+                    "(p e) f -> p e f", e=PAIR
+                ),
+                in_=result[:],
+            )
+
+        quantise(wo_sb, identity[:], wo_codes[:, 0:FEATURES], wo_scales[:, 0:FEATURES], E4M3_X4)
+
+        ready = prepare(0)
+        for band in range(1, BANDS):
+            following = prepare(band)
+            multiply_and_store(band - 1, ready[0], ready[1])
+            ready = following
+        multiply_and_store(BANDS - 1, ready[0], ready[1])

@@ -26,6 +26,7 @@ PAIRS_IN_WINDOW_ROW = WINDOW // PAIR
 HALVES = 2
 PACK = 4
 MOVING_COLUMNS = 512
+WARM_UP_PASSES = 8
 
 FLOPS = 2 * HEIGHT * WIDTH * FEATURES * CHANNELS
 BYTES = 2 * HEIGHT * WIDTH * CHANNELS + 2 * FEATURES * CHANNELS + 4 * HEIGHT * WIDTH * FEATURES
@@ -102,15 +103,27 @@ def tile_windowattentionblock_pb_s_kernel(tc, attn_ctx, x, wo, bo, grad_out, out
                 )
             band_pixels.append(pixels)
 
+        wo_codes = keep.tile([P, MOVING_COLUMNS], U32, align_bytes=64)
+        wo_scales = keep.tile([P, MOVING_COLUMNS], U8, align_bytes=64)
+        nc.vector.memset(wo_codes[:].bitcast(I32), 0)
+        nc.vector.memset(wo_scales[:].bitcast(I32), 0)
+
+        unread = psum.tile([P, MOVING_COLUMNS], F32, name="even_sums")
+        for warm_up_pass in range(WARM_UP_PASSES):
+            nc.tensor.matmul_mx(
+                out=unread[:],
+                lhsT=wo_codes[:, 0:P].bitcast(E5M2_X4),
+                lhsT_scale=wo_scales[:, 0:P],
+                rhs=wo_codes[:].bitcast(E4M3_X4),
+                rhs_scale=wo_scales[:],
+                start=True,
+                stop=True,
+            )
+
         identity = keep.tile([P, P], F32)
         make_identity(nc, identity[:])
         window_order = keep.tile([P, P], F32)
         make_window_order(nc, window_order[:], identity[:])
-
-        wo_codes = keep.tile([P, MOVING_COLUMNS], U32, align_bytes=64)
-        wo_scales = keep.tile([P, MOVING_COLUMNS], U8, align_bytes=64)
-        nc.vector.memset(wo_codes[:, FEATURES:MOVING_COLUMNS].bitcast(I32), 0)
-        nc.vector.memset(wo_scales[:, FEATURES:MOVING_COLUMNS].bitcast(I32), 0)
 
         def quantise(rows_sb, column_order, codes, scales, fp8_x4):
             grouped = bands.tile([P, PAIR, P * PACK], BF16, align_bytes=64, name="grouped")

@@ -18,54 +18,42 @@ CHANNELS = 512
 FEATURES = 256
 WINDOW = 8
 SHIFT = 4
+STRIP_ROWS = P // WIDTH
+STRIPS = HEIGHT // STRIP_ROWS
 BANDS = HEIGHT // WINDOW
+STRIPS_IN_BAND = STRIPS // BANDS
 WINDOWS_IN_BAND = WIDTH // WINDOW
-PAIR = 2
-PAIRS_IN_ROW = WIDTH // PAIR
-PAIRS_IN_WINDOW_ROW = WINDOW // PAIR
+PASSES_IN_BAND = WINDOWS_IN_BAND * WINDOW * WINDOW // P
+WO_TILES = FEATURES // P
 HALVES = 2
 PACK = 4
 MOVING_COLUMNS = 512
-WARM_UP_PASSES = 8
+PSUM_BANKS = 8
+
+assert SHIFT % STRIP_ROWS == 0
 
 FLOPS = 2 * HEIGHT * WIDTH * FEATURES * CHANNELS
 BYTES = 2 * HEIGHT * WIDTH * CHANNELS + 2 * FEATURES * CHANNELS + 4 * HEIGHT * WIDTH * FEATURES
 
 
 def make_window_order(nc, window_order, identity):
-    moved = SHIFT // PAIR
-    from_image = identity.rearrange("p (row pair) -> p row pair", pair=PAIRS_IN_ROW)
+    from_image = identity.rearrange("p (row col) -> p row col", col=WIDTH)
     to_window = window_order.rearrange(
-        "p (win row pair) -> p win row pair", win=WINDOWS_IN_BAND, row=WINDOW
+        "p (win row col) -> p win row col", win=WINDOWS_IN_BAND, row=STRIP_ROWS
     )
     last = WINDOWS_IN_BAND - 1
-    kept = PAIRS_IN_WINDOW_ROW - moved
     nc.vector.tensor_copy(
         out=to_window[:, 0:last],
-        in_=from_image[:, :, moved : moved + last * PAIRS_IN_WINDOW_ROW].rearrange(
-            "p row (win pair) -> p win row pair", pair=PAIRS_IN_WINDOW_ROW
+        in_=from_image[:, :, SHIFT : SHIFT + last * WINDOW].rearrange(
+            "p row (win col) -> p win row col", col=WINDOW
         ),
     )
     nc.vector.tensor_copy(
-        out=to_window[:, last, :, 0:kept], in_=from_image[:, :, PAIRS_IN_ROW - kept : PAIRS_IN_ROW]
+        out=to_window[:, last, :, 0 : WINDOW - SHIFT],
+        in_=from_image[:, :, SHIFT + last * WINDOW : WIDTH],
     )
     nc.vector.tensor_copy(
-        out=to_window[:, last, :, kept:PAIRS_IN_WINDOW_ROW], in_=from_image[:, :, 0:moved]
-    )
-
-
-def transpose_rows(nc, bank, rows, column_order):
-    words = rows.bitcast(F32)
-    for half in range(HALVES):
-        nc.tensor.transpose(
-            out=bank[:, half, :], in_=words[:, half * P : (half + 1) * P], identity=column_order
-        )
-
-
-def regroup(copy, grouped, bank):
-    copy(
-        out=grouped.bitcast(F32).rearrange("p (j half) -> p j half", half=HALVES),
-        in_=bank[:].rearrange("p half j -> p j half"),
+        out=to_window[:, last, :, WINDOW - SHIFT : WINDOW], in_=from_image[:, :, 0:SHIFT]
     )
 
 
@@ -75,104 +63,95 @@ def tile_windowattentionblock_pb_s_kernel(tc, attn_ctx, x, wo, bo, grad_out, out
     wo_rows = wo.rearrange("h d c -> (h d) c")
     out_rows = out.rearrange("n t h d -> (n t) (h d)")
 
-    with ExitStack() as pools:
-        keep = pools.enter_context(tc.tile_pool(name="keep", bufs=1))
-        bands = pools.enter_context(tc.tile_pool(name="bands", bufs=BANDS))
-        psum = pools.enter_context(tc.psum_pool(name="psum", bufs=2))
+    with ExitStack() as stack:
+        keep = stack.enter_context(tc.tile_pool(name="keep", bufs=1))
+        strips = stack.enter_context(tc.tile_pool(name="strips", bufs=STRIPS))
+        bands = stack.enter_context(tc.tile_pool(name="bands", bufs=BANDS))
+        results = stack.enter_context(tc.tile_pool(name="results", bufs=BANDS * PASSES_IN_BAND))
+        transposed = stack.enter_context(tc.psum_pool(name="transposed", bufs=PSUM_BANKS // 2))
+        products = stack.enter_context(tc.psum_pool(name="products", bufs=PSUM_BANKS // 2))
+        stack.enter_context(tc.manual_schedule())
 
-        wo_sb = keep.tile([P, PAIR, CHANNELS], BF16)
+        copy_out = (nc.vector.tensor_copy, nc.scalar.copy)
+
+        wo_sb = keep.tile([P, WO_TILES, CHANNELS], BF16)
         nc.sync.dma_start(out=wo_sb[:], in_=wo_rows.rearrange("(a p) c -> p a c", p=P))
-        band_pixels = []
+        band_strips = []
         for band in range(BANDS):
-            pixels = bands.tile([P, PAIR, CHANNELS], BF16, name="pixels")
-            first_row = WINDOW * band + SHIFT
-            rows_above_edge = min(WINDOW, HEIGHT - first_row)
-            split = rows_above_edge * PAIRS_IN_ROW
-            nc.sync.dma_start(
-                out=pixels[0:split],
-                in_=image[first_row * WIDTH : (first_row + rows_above_edge) * WIDTH].rearrange(
-                    "(p e) c -> p e c", e=PAIR
-                ),
-            )
-            if split < P:
-                nc.sync.dma_start(
-                    out=pixels[split:P],
-                    in_=image[0 : (WINDOW - rows_above_edge) * WIDTH].rearrange(
-                        "(p e) c -> p e c", e=PAIR
-                    ),
-                )
-            band_pixels.append(pixels)
+            for h in range(STRIPS_IN_BAND):
+                strip = (band * STRIPS_IN_BAND + h + SHIFT // STRIP_ROWS) % STRIPS
+                pixels = strips.tile([P, CHANNELS], BF16, name="pixels")
+                nc.sync.dma_start(out=pixels[:], in_=image[strip * P : (strip + 1) * P])
+                band_strips.append(pixels)
 
         wo_codes = keep.tile([P, MOVING_COLUMNS], U32, align_bytes=64)
         wo_scales = keep.tile([P, MOVING_COLUMNS], U8, align_bytes=64)
-        nc.vector.memset(wo_codes[:].bitcast(I32), 0)
-        nc.vector.memset(wo_scales[:].bitcast(I32), 0)
-
-        unread = psum.tile([P, MOVING_COLUMNS], F32, name="even_sums")
-        for warm_up_pass in range(WARM_UP_PASSES):
-            nc.tensor.matmul_mx(
-                out=unread[:],
-                lhsT=wo_codes[:, 0:P].bitcast(E5M2_X4),
-                lhsT_scale=wo_scales[:, 0:P],
-                rhs=wo_codes[:].bitcast(E4M3_X4),
-                rhs_scale=wo_scales[:],
-                start=True,
-                stop=True,
-            )
+        nc.vector.memset(wo_codes[:, FEATURES:MOVING_COLUMNS].bitcast(I32), 0)
+        nc.vector.memset(wo_scales[:, FEATURES:MOVING_COLUMNS].bitcast(I32), 0)
 
         identity = keep.tile([P, P], F32)
         make_identity(nc, identity[:])
         window_order = keep.tile([P, P], F32)
         make_window_order(nc, window_order[:], identity[:])
 
-        def quantise(rows_sb, column_order, codes, scales, fp8_x4):
-            grouped = bands.tile([P, PAIR, P * PACK], BF16, align_bytes=64, name="grouped")
-            even_bank = psum.tile([P, HALVES, P], F32, name="even_bank")
-            odd_bank = psum.tile([P, HALVES, P], F32, name="odd_bank")
-            transpose_rows(nc, even_bank, rows_sb[:, 0, :], column_order)
-            transpose_rows(nc, odd_bank, rows_sb[:, 1, :], column_order)
-            regroup(nc.vector.tensor_copy, grouped[:, 0, :], even_bank)
-            regroup(nc.scalar.copy, grouped[:, 1, :], odd_bank)
-            nc.vector.quantize_mx(
-                out=codes.bitcast(fp8_x4),
-                scales=scales,
-                in_=grouped[:].rearrange("p e v -> p (e v)"),
+        def transpose_rows(rows, column_order):
+            bank = transposed.tile([P, HALVES, P], F32, name="bank")
+            words = rows.bitcast(F32)
+            for half in range(HALVES):
+                nc.tensor.transpose(
+                    out=bank[:, half, :],
+                    in_=words[:, half * P : (half + 1) * P],
+                    identity=column_order,
+                )
+            return bank
+
+        wo_grouped = keep.tile([P, FEATURES * PACK], BF16, align_bytes=64)
+        wo_words = wo_grouped[:].bitcast(F32).rearrange(
+            "p (a j half) -> p a j half", a=WO_TILES, half=HALVES
+        )
+        for a in range(WO_TILES):
+            bank = transpose_rows(wo_sb[:, a, :], identity[:])
+            copy_out[a % 2](out=wo_words[:, a], in_=bank[:].rearrange("p half j -> p j half"))
+        nc.vector.quantize_mx(
+            out=wo_codes[:, 0:FEATURES].bitcast(E4M3_X4),
+            scales=wo_scales[:, 0:FEATURES],
+            in_=wo_grouped[:],
+        )
+
+        band_codes = []
+        for band in range(BANDS):
+            grouped = bands.tile([P, PASSES_IN_BAND * P * PACK], BF16, align_bytes=64, name="grouped")
+            codes = bands.tile([P, PASSES_IN_BAND * P], U32, align_bytes=64, name="codes")
+            scales = bands.tile([P, PASSES_IN_BAND * P], U8, align_bytes=64, name="scales")
+            words = grouped[:].bitcast(F32).rearrange(
+                "p (win h j half) -> p h win j half",
+                win=WINDOWS_IN_BAND,
+                h=STRIPS_IN_BAND,
+                half=HALVES,
             )
+            for h in range(STRIPS_IN_BAND):
+                bank = transpose_rows(band_strips[band * STRIPS_IN_BAND + h][:], window_order[:])
+                copy_out[h % 2](
+                    out=words[:, h],
+                    in_=bank[:].rearrange("p half (win j) -> p win j half", win=WINDOWS_IN_BAND),
+                )
+            nc.vector.quantize_mx(out=codes[:].bitcast(E5M2_X4), scales=scales[:], in_=grouped[:])
+            band_codes.append((codes, scales))
 
-        def prepare(band):
-            codes = bands.tile([P, PAIR * P], U32, align_bytes=64, name="codes")
-            scales = bands.tile([P, PAIR * P], U8, align_bytes=64, name="scales")
-            quantise(band_pixels[band], window_order[:], codes[:], scales[:], E5M2_X4)
-            return codes, scales
-
-        def multiply_and_store(band, codes, scales):
-            result = bands.tile([P, PAIR, FEATURES], F32, name="result")
-            even_sums = psum.tile([P, MOVING_COLUMNS], F32, name="even_sums")
-            odd_sums = psum.tile([P, MOVING_COLUMNS], F32, name="odd_sums")
-            for e, sums in enumerate((even_sums, odd_sums)):
+        for band in range(BANDS):
+            codes, scales = band_codes[band]
+            for w in range(PASSES_IN_BAND):
+                sums = products.tile([P, MOVING_COLUMNS], F32, name="sums")
                 nc.tensor.matmul_mx(
                     out=sums[:],
-                    lhsT=codes[:, e * P : (e + 1) * P].bitcast(E5M2_X4),
-                    lhsT_scale=scales[:, e * P : (e + 1) * P],
+                    lhsT=codes[:, w * P : (w + 1) * P].bitcast(E5M2_X4),
+                    lhsT_scale=scales[:, w * P : (w + 1) * P],
                     rhs=wo_codes[:].bitcast(E4M3_X4),
                     rhs_scale=wo_scales[:],
                     start=True,
                     stop=True,
                 )
-            nc.vector.tensor_copy(out=result[:, 0, :], in_=even_sums[:, 0:FEATURES])
-            nc.scalar.copy(out=result[:, 1, :], in_=odd_sums[:, 0:FEATURES])
-            nc.sync.dma_start(
-                out=out_rows[band * PAIR * P : (band + 1) * PAIR * P].rearrange(
-                    "(p e) f -> p e f", e=PAIR
-                ),
-                in_=result[:],
-            )
-
-        quantise(wo_sb, identity[:], wo_codes[:, 0:FEATURES], wo_scales[:, 0:FEATURES], E4M3_X4)
-
-        ready = prepare(0)
-        for band in range(1, BANDS):
-            following = prepare(band)
-            multiply_and_store(band - 1, ready[0], ready[1])
-            ready = following
-        multiply_and_store(BANDS - 1, ready[0], ready[1])
+                result = results.tile([P, FEATURES], F32, name="result")
+                copy_out[w % 2](out=result[:], in_=sums[:, 0:FEATURES])
+                first_row = (band * PASSES_IN_BAND + w) * P
+                nc.sync.dma_start(out=out_rows[first_row : first_row + P], in_=result[:])

@@ -29,6 +29,7 @@ HALVES = 2
 PACK = 4
 MOVING_COLUMNS = 512
 PSUM_BANKS = 8
+WARM_UP_PASSES = 4
 
 assert SHIFT % STRIP_ROWS == 0
 
@@ -86,8 +87,20 @@ def tile_windowattentionblock_pb_s_kernel(tc, attn_ctx, x, wo, bo, grad_out, out
 
         wo_codes = keep.tile([P, MOVING_COLUMNS], U32, align_bytes=64)
         wo_scales = keep.tile([P, MOVING_COLUMNS], U8, align_bytes=64)
-        nc.vector.memset(wo_codes[:, FEATURES:MOVING_COLUMNS].bitcast(I32), 0)
-        nc.vector.memset(wo_scales[:, FEATURES:MOVING_COLUMNS].bitcast(I32), 0)
+        nc.vector.memset(wo_codes[:].bitcast(I32), 0)
+        nc.vector.memset(wo_scales[:].bitcast(I32), 0)
+
+        unread = products.tile([P, MOVING_COLUMNS], F32, name="sums")
+        for warm_up_pass in range(WARM_UP_PASSES):
+            nc.tensor.matmul_mx(
+                out=unread[:],
+                lhsT=wo_codes[:, 0:P].bitcast(E5M2_X4),
+                lhsT_scale=wo_scales[:, 0:P],
+                rhs=wo_codes[:].bitcast(E4M3_X4),
+                rhs_scale=wo_scales[:],
+                start=True,
+                stop=True,
+            )
 
         identity = keep.tile([P, P], F32)
         make_identity(nc, identity[:])

@@ -29,7 +29,6 @@ HALVES = 2
 PACK = 4
 MOVING_COLUMNS = 512
 PSUM_BANKS = 8
-WARM_UP_PASSES = 4
 
 assert SHIFT % STRIP_ROWS == 0
 
@@ -75,32 +74,24 @@ def tile_windowattentionblock_pb_s_kernel(tc, attn_ctx, x, wo, bo, grad_out, out
 
         copy_out = (nc.vector.tensor_copy, nc.scalar.copy)
 
-        wo_sb = keep.tile([P, WO_TILES, CHANNELS], BF16)
-        nc.sync.dma_start(out=wo_sb[:], in_=wo_rows.rearrange("(a p) c -> p a c", p=P))
-        band_strips = []
-        for band in range(BANDS):
+        def load_band(band):
             for h in range(STRIPS_IN_BAND):
                 strip = (band * STRIPS_IN_BAND + h + SHIFT // STRIP_ROWS) % STRIPS
                 pixels = strips.tile([P, CHANNELS], BF16, name="pixels")
                 nc.sync.dma_start(out=pixels[:], in_=image[strip * P : (strip + 1) * P])
                 band_strips.append(pixels)
 
+        band_strips = []
+        wo_sb = keep.tile([P, WO_TILES, CHANNELS], BF16)
+        load_band(0)
+        nc.sync.dma_start(out=wo_sb[:], in_=wo_rows.rearrange("(a p) c -> p a c", p=P))
+        for band in range(1, BANDS):
+            load_band(band)
+
         wo_codes = keep.tile([P, MOVING_COLUMNS], U32, align_bytes=64)
         wo_scales = keep.tile([P, MOVING_COLUMNS], U8, align_bytes=64)
-        nc.vector.memset(wo_codes[:].bitcast(I32), 0)
-        nc.vector.memset(wo_scales[:].bitcast(I32), 0)
-
-        unread = products.tile([P, MOVING_COLUMNS], F32, name="sums")
-        for warm_up_pass in range(WARM_UP_PASSES):
-            nc.tensor.matmul_mx(
-                out=unread[:],
-                lhsT=wo_codes[:, 0:P].bitcast(E5M2_X4),
-                lhsT_scale=wo_scales[:, 0:P],
-                rhs=wo_codes[:].bitcast(E4M3_X4),
-                rhs_scale=wo_scales[:],
-                start=True,
-                stop=True,
-            )
+        nc.vector.memset(wo_codes[:, FEATURES:MOVING_COLUMNS].bitcast(I32), 0)
+        nc.vector.memset(wo_scales[:, FEATURES:MOVING_COLUMNS].bitcast(I32), 0)
 
         identity = keep.tile([P, P], F32)
         make_identity(nc, identity[:])
@@ -118,21 +109,21 @@ def tile_windowattentionblock_pb_s_kernel(tc, attn_ctx, x, wo, bo, grad_out, out
                 )
             return bank
 
-        wo_grouped = keep.tile([P, FEATURES * PACK], BF16, align_bytes=64)
-        wo_words = wo_grouped[:].bitcast(F32).rearrange(
-            "p (a j half) -> p a j half", a=WO_TILES, half=HALVES
-        )
-        for a in range(WO_TILES):
-            bank = transpose_rows(wo_sb[:, a, :], identity[:])
-            copy_out[a % 2](out=wo_words[:, a], in_=bank[:].rearrange("p half j -> p j half"))
-        nc.vector.quantize_mx(
-            out=wo_codes[:, 0:FEATURES].bitcast(E4M3_X4),
-            scales=wo_scales[:, 0:FEATURES],
-            in_=wo_grouped[:],
-        )
+        def quantise_wo():
+            wo_grouped = keep.tile([P, FEATURES * PACK], BF16, align_bytes=64)
+            wo_words = wo_grouped[:].bitcast(F32).rearrange(
+                "p (a j half) -> p a j half", a=WO_TILES, half=HALVES
+            )
+            for a in range(WO_TILES):
+                bank = transpose_rows(wo_sb[:, a, :], identity[:])
+                copy_out[a % 2](out=wo_words[:, a], in_=bank[:].rearrange("p half j -> p j half"))
+            nc.vector.quantize_mx(
+                out=wo_codes[:, 0:FEATURES].bitcast(E4M3_X4),
+                scales=wo_scales[:, 0:FEATURES],
+                in_=wo_grouped[:],
+            )
 
-        band_codes = []
-        for band in range(BANDS):
+        def quantise_band(band):
             grouped = bands.tile([P, PASSES_IN_BAND * P * PACK], BF16, align_bytes=64, name="grouped")
             codes = bands.tile([P, PASSES_IN_BAND * P], U32, align_bytes=64, name="codes")
             scales = bands.tile([P, PASSES_IN_BAND * P], U8, align_bytes=64, name="scales")
@@ -150,6 +141,12 @@ def tile_windowattentionblock_pb_s_kernel(tc, attn_ctx, x, wo, bo, grad_out, out
                 )
             nc.vector.quantize_mx(out=codes[:].bitcast(E5M2_X4), scales=scales[:], in_=grouped[:])
             band_codes.append((codes, scales))
+
+        band_codes = []
+        quantise_band(0)
+        quantise_wo()
+        for band in range(1, BANDS):
+            quantise_band(band)
 
         for band in range(BANDS):
             codes, scales = band_codes[band]

@@ -68,8 +68,7 @@ def tile_windowattentionblock_pb_s_kernel(tc, attn_ctx, x, wo, bo, grad_out, out
         strips = stack.enter_context(tc.tile_pool(name="strips", bufs=STRIPS))
         bands = stack.enter_context(tc.tile_pool(name="bands", bufs=BANDS))
         results = stack.enter_context(tc.tile_pool(name="results", bufs=BANDS * PASSES_IN_BAND))
-        transposed = stack.enter_context(tc.psum_pool(name="transposed", bufs=PSUM_BANKS // 2))
-        products = stack.enter_context(tc.psum_pool(name="products", bufs=PSUM_BANKS // 2))
+        banks = stack.enter_context(tc.psum_pool(name="banks", bufs=PSUM_BANKS))
         stack.enter_context(tc.manual_schedule())
 
         copy_out = (nc.vector.tensor_copy, nc.scalar.copy)
@@ -99,7 +98,8 @@ def tile_windowattentionblock_pb_s_kernel(tc, attn_ctx, x, wo, bo, grad_out, out
         make_window_order(nc, window_order[:], identity[:])
 
         def transpose_rows(rows, column_order):
-            bank = transposed.tile([P, HALVES, P], F32, name="bank")
+            whole_bank = banks.tile([P, MOVING_COLUMNS], F32, name="bank")
+            bank = whole_bank[:, 0 : HALVES * P].rearrange("p (half j) -> p half j", half=HALVES)
             words = rows.bitcast(F32)
             for half in range(HALVES):
                 nc.tensor.transpose(
@@ -109,24 +109,25 @@ def tile_windowattentionblock_pb_s_kernel(tc, attn_ctx, x, wo, bo, grad_out, out
                 )
             return bank
 
-        def quantise_wo():
-            wo_grouped = keep.tile([P, FEATURES * PACK], BF16, align_bytes=64)
+        wo_grouped = keep.tile([P, FEATURES * PACK], BF16, align_bytes=64)
+
+        def transpose_wo():
             wo_words = wo_grouped[:].bitcast(F32).rearrange(
                 "p (a j half) -> p a j half", a=WO_TILES, half=HALVES
             )
             for a in range(WO_TILES):
                 bank = transpose_rows(wo_sb[:, a, :], identity[:])
-                copy_out[a % 2](out=wo_words[:, a], in_=bank[:].rearrange("p half j -> p j half"))
+                copy_out[a % 2](out=wo_words[:, a], in_=bank.rearrange("p half j -> p j half"))
+
+        def quantise_wo():
             nc.vector.quantize_mx(
                 out=wo_codes[:, 0:FEATURES].bitcast(E4M3_X4),
                 scales=wo_scales[:, 0:FEATURES],
                 in_=wo_grouped[:],
             )
 
-        def quantise_band(band):
+        def transpose_band(band):
             grouped = bands.tile([P, PASSES_IN_BAND * P * PACK], BF16, align_bytes=64, name="grouped")
-            codes = bands.tile([P, PASSES_IN_BAND * P], U32, align_bytes=64, name="codes")
-            scales = bands.tile([P, PASSES_IN_BAND * P], U8, align_bytes=64, name="scales")
             words = grouped[:].bitcast(F32).rearrange(
                 "p (win h j half) -> p h win j half",
                 win=WINDOWS_IN_BAND,
@@ -137,21 +138,34 @@ def tile_windowattentionblock_pb_s_kernel(tc, attn_ctx, x, wo, bo, grad_out, out
                 bank = transpose_rows(band_strips[band * STRIPS_IN_BAND + h][:], window_order[:])
                 copy_out[h % 2](
                     out=words[:, h],
-                    in_=bank[:].rearrange("p half (win j) -> p win j half", win=WINDOWS_IN_BAND),
+                    in_=bank.rearrange("p half (win j) -> p win j half", win=WINDOWS_IN_BAND),
                 )
-            nc.vector.quantize_mx(out=codes[:].bitcast(E5M2_X4), scales=scales[:], in_=grouped[:])
+            band_grouped.append(grouped)
+
+        def quantise_band(band):
+            codes = bands.tile([P, PASSES_IN_BAND * P], U32, align_bytes=64, name="codes")
+            scales = bands.tile([P, PASSES_IN_BAND * P], U8, align_bytes=64, name="scales")
+            nc.vector.quantize_mx(
+                out=codes[:].bitcast(E5M2_X4), scales=scales[:], in_=band_grouped[band][:]
+            )
             band_codes.append((codes, scales))
 
+        band_grouped = []
         band_codes = []
+        transpose_band(0)
+        transpose_wo()
         quantise_band(0)
+        transpose_band(1)
         quantise_wo()
-        for band in range(1, BANDS):
-            quantise_band(band)
+        for band in range(2, BANDS):
+            transpose_band(band)
+            quantise_band(band - 1)
+        quantise_band(BANDS - 1)
 
         for band in range(BANDS):
             codes, scales = band_codes[band]
             for w in range(PASSES_IN_BAND):
-                sums = products.tile([P, MOVING_COLUMNS], F32, name="sums")
+                sums = banks.tile([P, MOVING_COLUMNS], F32, name="bank")
                 nc.tensor.matmul_mx(
                     out=sums[:],
                     lhsT=codes[:, w * P : (w + 1) * P].bitcast(E5M2_X4),

@@ -176,6 +176,6 @@ def tile_windowattentionblock_pb_s_kernel(tc, attn_ctx, x, wo, bo, grad_out, out
                     stop=True,
                 )
                 result = results.tile([P, FEATURES], F32, name="result")
-                copy_out[w % 2](out=result[:], in_=sums[:, 0:FEATURES])
+                copy_out[(w + 1) % 2](out=result[:], in_=sums[:, 0:FEATURES])
                 first_row = (band * PASSES_IN_BAND + w) * P
                 nc.sync.dma_start(out=out_rows[first_row : first_row + P], in_=result[:])

@@ -18,43 +18,67 @@ CHANNELS = 512
 FEATURES = 256
 WINDOW = 8
 SHIFT = 4
-STRIP_ROWS = P // WIDTH
-STRIPS = HEIGHT // STRIP_ROWS
 BANDS = HEIGHT // WINDOW
-STRIPS_IN_BAND = STRIPS // BANDS
-WINDOWS_IN_BAND = WIDTH // WINDOW
-PASSES_IN_BAND = WINDOWS_IN_BAND * WINDOW * WINDOW // P
-WO_TILES = FEATURES // P
+WINDOWS = WIDTH // WINDOW
+BAND_PIXELS = WINDOW * WIDTH
+PAIR = BAND_PIXELS // P
+STRIP_ROWS = P // WIDTH
+STRIPS = BAND_PIXELS // P
 HALVES = 2
 PACK = 4
 MOVING_COLUMNS = 512
 PSUM_BANKS = 8
-
-assert SHIFT % STRIP_ROWS == 0
+WARM_COLUMNS = 136
 
 FLOPS = 2 * HEIGHT * WIDTH * FEATURES * CHANNELS
 BYTES = 2 * HEIGHT * WIDTH * CHANNELS + 2 * FEATURES * CHANNELS + 4 * HEIGHT * WIDTH * FEATURES
 
 
-def make_window_order(nc, window_order, identity):
-    from_image = identity.rearrange("p (row col) -> p row col", col=WIDTH)
-    to_window = window_order.rearrange(
-        "p (win row col) -> p win row col", win=WINDOWS_IN_BAND, row=STRIP_ROWS
-    )
-    last = WINDOWS_IN_BAND - 1
+def make_pair_order(nc, pair_order, identity):
+    pairs = WIDTH // PAIR
+    in_window = WINDOW // PAIR
+    shift = SHIFT // PAIR
+    from_image = identity.rearrange("p (row pair) -> p row pair", pair=pairs)
+    to_window = pair_order.rearrange("p (win row pair) -> p win row pair", win=WINDOWS, pair=in_window)
+    last = WINDOWS - 1
     nc.vector.tensor_copy(
         out=to_window[:, 0:last],
-        in_=from_image[:, :, SHIFT : SHIFT + last * WINDOW].rearrange(
-            "p row (win col) -> p win row col", col=WINDOW
+        in_=from_image[:, :, shift : shift + last * in_window].rearrange(
+            "p row (win pair) -> p win row pair", pair=in_window
         ),
     )
     nc.vector.tensor_copy(
-        out=to_window[:, last, :, 0 : WINDOW - SHIFT],
-        in_=from_image[:, :, SHIFT + last * WINDOW : WIDTH],
+        out=to_window[:, last, :, 0 : in_window - shift],
+        in_=from_image[:, :, shift + last * in_window : pairs],
     )
     nc.vector.tensor_copy(
-        out=to_window[:, last, :, WINDOW - SHIFT : WINDOW], in_=from_image[:, :, 0:SHIFT]
+        out=to_window[:, last, :, in_window - shift : in_window], in_=from_image[:, :, 0:shift]
     )
+
+
+def make_strip_order(nc, strip_order, identity):
+    in_window = WINDOW // PAIR
+    from_image = identity.rearrange("p (row col) -> p row col", col=WIDTH)
+    to_window = strip_order.rearrange(
+        "p (e win row pair) -> p e win row pair", e=PAIR, win=WINDOWS, pair=in_window
+    )
+    last = WINDOWS - 1
+    wrap = SHIFT + last * WINDOW
+    for e in range(PAIR):
+        nc.vector.tensor_copy(
+            out=to_window[:, e, 0:last],
+            in_=from_image[:, :, SHIFT + e : wrap + e : PAIR].rearrange(
+                "p row (win pair) -> p win row pair", pair=in_window
+            ),
+        )
+        nc.vector.tensor_copy(
+            out=to_window[:, e, last, :, 0 : (WIDTH - wrap) // PAIR],
+            in_=from_image[:, :, wrap + e : WIDTH : PAIR],
+        )
+        nc.vector.tensor_copy(
+            out=to_window[:, e, last, :, (WIDTH - wrap) // PAIR : in_window],
+            in_=from_image[:, :, e : SHIFT : PAIR],
+        )
 
 
 def tile_windowattentionblock_pb_s_kernel(tc, attn_ctx, x, wo, bo, grad_out, out):
@@ -65,27 +89,43 @@ def tile_windowattentionblock_pb_s_kernel(tc, attn_ctx, x, wo, bo, grad_out, out
 
     with ExitStack() as stack:
         keep = stack.enter_context(tc.tile_pool(name="keep", bufs=1))
-        strips = stack.enter_context(tc.tile_pool(name="strips", bufs=STRIPS))
-        bands = stack.enter_context(tc.tile_pool(name="bands", bufs=BANDS))
-        results = stack.enter_context(tc.tile_pool(name="results", bufs=BANDS * PASSES_IN_BAND))
+        bands = stack.enter_context(tc.tile_pool(name="bands", bufs=BANDS + 1))
+        results = stack.enter_context(tc.tile_pool(name="results", bufs=BANDS * PAIR))
         banks = stack.enter_context(tc.psum_pool(name="banks", bufs=PSUM_BANKS))
         stack.enter_context(tc.manual_schedule())
 
         copy_out = (nc.vector.tensor_copy, nc.scalar.copy)
 
-        def load_band(band):
-            for h in range(STRIPS_IN_BAND):
-                strip = (band * STRIPS_IN_BAND + h + SHIFT // STRIP_ROWS) % STRIPS
-                pixels = strips.tile([P, CHANNELS], BF16, name="pixels")
-                nc.sync.dma_start(out=pixels[:], in_=image[strip * P : (strip + 1) * P])
-                band_strips.append(pixels)
+        ones = keep.tile([P, WARM_COLUMNS], F32)
+        nc.gpsimd.memset(ones[:], 1.0)
 
-        band_strips = []
-        wo_sb = keep.tile([P, WO_TILES, CHANNELS], BF16)
-        load_band(0)
-        nc.sync.dma_start(out=wo_sb[:], in_=wo_rows.rearrange("(a p) c -> p a c", p=P))
-        for band in range(1, BANDS):
-            load_band(band)
+        def keep_busy(stationary):
+            unread = banks.tile([P, MOVING_COLUMNS], F32, name="bank")
+            nc.tensor.matmul(
+                out=unread[:, 0:WARM_COLUMNS], lhsT=stationary, rhs=ones[:], start=True, stop=True
+            )
+
+        keep_busy(ones[:, 0:P])
+
+        def load_pairs(rows):
+            pair = bands.tile([P, PAIR, CHANNELS], BF16, name="pair")
+            nc.sync.dma_start(out=pair[:], in_=rows.rearrange("(p e) c -> p e c", e=PAIR))
+            return pair
+
+        def band_start(band):
+            return (band * WINDOW + SHIFT) * WIDTH
+
+        whole_bands = BANDS - 1
+        band_pairs = [load_pairs(image[band_start(0) : band_start(0) + BAND_PIXELS])]
+        wo_pairs = load_pairs(wo_rows)
+        for band in range(1, whole_bands):
+            band_pairs.append(load_pairs(image[band_start(band) : band_start(band) + BAND_PIXELS]))
+        last_strips = []
+        for h in range(STRIPS):
+            first = (band_start(whole_bands) + h * P) % (HEIGHT * WIDTH)
+            strip = keep.tile([P, CHANNELS], BF16, name="strip%d" % h)
+            nc.sync.dma_start(out=strip[:], in_=image[first : first + P])
+            last_strips.append(strip)
 
         wo_codes = keep.tile([P, MOVING_COLUMNS], U32, align_bytes=64)
         wo_scales = keep.tile([P, MOVING_COLUMNS], U8, align_bytes=64)
@@ -94,8 +134,12 @@ def tile_windowattentionblock_pb_s_kernel(tc, attn_ctx, x, wo, bo, grad_out, out
 
         identity = keep.tile([P, P], F32)
         make_identity(nc, identity[:])
-        window_order = keep.tile([P, P], F32)
-        make_window_order(nc, window_order[:], identity[:])
+        keep_busy(identity[:])
+        pair_order = keep.tile([P, P], F32)
+        make_pair_order(nc, pair_order[:], identity[:])
+        keep_busy(pair_order[:])
+        strip_order = keep.tile([P, P], F32)
+        make_strip_order(nc, strip_order[:], identity[:])
 
         def transpose_rows(rows, column_order):
             whole_bank = banks.tile([P, MOVING_COLUMNS], F32, name="bank")
@@ -109,73 +153,74 @@ def tile_windowattentionblock_pb_s_kernel(tc, attn_ctx, x, wo, bo, grad_out, out
                 )
             return bank
 
-        wo_grouped = keep.tile([P, FEATURES * PACK], BF16, align_bytes=64)
+        def transpose_pairs(pair, column_order):
+            grouped = bands.tile([P, PAIR * P * PACK], BF16, align_bytes=64, name="grouped")
+            words = grouped[:].bitcast(F32).rearrange("p (e m half) -> p e m half", e=PAIR, half=HALVES)
+            for e in range(PAIR):
+                bank = transpose_rows(pair[:, e, :], column_order)
+                copy_out[e % 2](out=words[:, e], in_=bank.rearrange("p half m -> p m half"))
+            return grouped
 
-        def transpose_wo():
-            wo_words = wo_grouped[:].bitcast(F32).rearrange(
-                "p (a j half) -> p a j half", a=WO_TILES, half=HALVES
+        def transpose_strips(strips):
+            grouped = bands.tile([P, PAIR * P * PACK], BF16, align_bytes=64, name="grouped")
+            words = grouped[:].bitcast(F32).rearrange(
+                "p (g h q half) -> p h g q half", g=PAIR * WINDOWS, h=STRIPS, half=HALVES
             )
-            for a in range(WO_TILES):
-                bank = transpose_rows(wo_sb[:, a, :], identity[:])
-                copy_out[a % 2](out=wo_words[:, a], in_=bank.rearrange("p half j -> p j half"))
+            for h in range(STRIPS):
+                bank = transpose_rows(strips[h][:], strip_order[:])
+                copy_out[h % 2](
+                    out=words[:, h],
+                    in_=bank.rearrange("p half (g q) -> p g q half", g=PAIR * WINDOWS),
+                )
+            return grouped
 
-        def quantise_wo():
+        def quantise_wo(grouped):
             nc.vector.quantize_mx(
                 out=wo_codes[:, 0:FEATURES].bitcast(E4M3_X4),
                 scales=wo_scales[:, 0:FEATURES],
-                in_=wo_grouped[:],
+                in_=grouped[:],
             )
 
-        def transpose_band(band):
-            grouped = bands.tile([P, PASSES_IN_BAND * P * PACK], BF16, align_bytes=64, name="grouped")
-            words = grouped[:].bitcast(F32).rearrange(
-                "p (win h j half) -> p h win j half",
-                win=WINDOWS_IN_BAND,
-                h=STRIPS_IN_BAND,
-                half=HALVES,
-            )
-            for h in range(STRIPS_IN_BAND):
-                bank = transpose_rows(band_strips[band * STRIPS_IN_BAND + h][:], window_order[:])
-                copy_out[h % 2](
-                    out=words[:, h],
-                    in_=bank.rearrange("p half (win j) -> p win j half", win=WINDOWS_IN_BAND),
-                )
-            band_grouped.append(grouped)
-
-        def quantise_band(band):
-            codes = bands.tile([P, PASSES_IN_BAND * P], U32, align_bytes=64, name="codes")
-            scales = bands.tile([P, PASSES_IN_BAND * P], U8, align_bytes=64, name="scales")
-            nc.vector.quantize_mx(
-                out=codes[:].bitcast(E5M2_X4), scales=scales[:], in_=band_grouped[band][:]
-            )
+        def quantise_band(grouped):
+            codes = bands.tile([P, PAIR * P], U32, align_bytes=64, name="codes")
+            scales = bands.tile([P, PAIR * P], U8, align_bytes=64, name="scales")
+            nc.vector.quantize_mx(out=codes[:].bitcast(E5M2_X4), scales=scales[:], in_=grouped[:])
             band_codes.append((codes, scales))
 
-        band_grouped = []
         band_codes = []
-        transpose_band(0)
-        transpose_wo()
-        quantise_band(0)
-        transpose_band(1)
-        quantise_wo()
-        for band in range(2, BANDS):
-            transpose_band(band)
-            quantise_band(band - 1)
-        quantise_band(BANDS - 1)
+        grouped_0 = transpose_pairs(band_pairs[0], pair_order[:])
+        keep_busy(ones[:, 0:P])
+        grouped_wo = transpose_pairs(wo_pairs, identity[:])
+        keep_busy(ones[:, 0:P])
+        quantise_band(grouped_0)
+        grouped_1 = transpose_pairs(band_pairs[1], pair_order[:])
+        quantise_wo(grouped_wo)
+        grouped_2 = transpose_pairs(band_pairs[2], pair_order[:])
+        keep_busy(ones[:, 0:P])
+        quantise_band(grouped_1)
+        grouped_3 = transpose_strips(last_strips)
+        quantise_band(grouped_2)
+        quantise_band(grouped_3)
 
         for band in range(BANDS):
             codes, scales = band_codes[band]
-            for w in range(PASSES_IN_BAND):
+            rows = out_rows[band * BAND_PIXELS : (band + 1) * BAND_PIXELS].rearrange(
+                "(m e) f -> m e f", e=PAIR
+            )
+            for e in range(PAIR):
                 sums = banks.tile([P, MOVING_COLUMNS], F32, name="bank")
                 nc.tensor.matmul_mx(
                     out=sums[:],
-                    lhsT=codes[:, w * P : (w + 1) * P].bitcast(E5M2_X4),
-                    lhsT_scale=scales[:, w * P : (w + 1) * P],
+                    lhsT=codes[:, e * P : (e + 1) * P].bitcast(E5M2_X4),
+                    lhsT_scale=scales[:, e * P : (e + 1) * P],
                     rhs=wo_codes[:].bitcast(E4M3_X4),
                     rhs_scale=wo_scales[:],
                     start=True,
                     stop=True,
                 )
                 result = results.tile([P, FEATURES], F32, name="result")
-                copy_out[(w + 1) % 2](out=result[:], in_=sums[:, 0:FEATURES])
-                first_row = (band * PASSES_IN_BAND + w) * P
-                nc.sync.dma_start(out=out_rows[first_row : first_row + P], in_=result[:])
+                copy_out[(e + 1) % 2](
+                    out=result[:].rearrange("p (m2 e2) -> p m2 e2", e2=PAIR),
+                    in_=sums[:, 0:FEATURES].rearrange("p (e2 m2) -> p m2 e2", e2=PAIR),
+                )
+                nc.sync.dma_start(out=rows[:, e, :], in_=result[:])

@@ -95,6 +95,7 @@ def tile_windowattentionblock_pb_s_kernel(tc, attn_ctx, x, wo, bo, grad_out, out
         stack.enter_context(tc.manual_schedule())
 
         copy_out = (nc.vector.tensor_copy, nc.scalar.copy)
+        store_queue = (nc.sync, nc.scalar)
 
         ones = keep.tile([P, WARM_COLUMNS], F32)
         nc.gpsimd.memset(ones[:], 1.0)
@@ -223,4 +224,4 @@ def tile_windowattentionblock_pb_s_kernel(tc, attn_ctx, x, wo, bo, grad_out, out
                     out=result[:].rearrange("p (m2 e2) -> p m2 e2", e2=PAIR),
                     in_=sums[:, 0:FEATURES].rearrange("p (e2 m2) -> p m2 e2", e2=PAIR),
                 )
-                nc.sync.dma_start(out=rows[:, e, :], in_=result[:])
+                store_queue[(e + 1) % 2].dma_start(out=rows[:, e, :], in_=result[:])

@@ -195,9 +195,9 @@ def tile_windowattentionblock_pb_s_kernel(tc, attn_ctx, x, wo, bo, grad_out, out
         keep_busy(ones[:, 0:P])
         quantise_band(grouped_0)
         grouped_1 = transpose_pairs(band_pairs[1], pair_order[:])
+        keep_busy(ones[:, 0:P])
         quantise_wo(grouped_wo)
         grouped_2 = transpose_pairs(band_pairs[2], pair_order[:])
-        keep_busy(ones[:, 0:P])
         quantise_band(grouped_1)
         grouped_3 = transpose_strips(last_strips)
         quantise_band(grouped_2)

@@ -94,8 +94,7 @@ def tile_windowattentionblock_pb_s_kernel(tc, attn_ctx, x, wo, bo, grad_out, out
         banks = stack.enter_context(tc.psum_pool(name="banks", bufs=PSUM_BANKS))
         stack.enter_context(tc.manual_schedule())
 
-        copy_out = (nc.vector.tensor_copy, nc.scalar.copy)
-        store_queue = (nc.sync, nc.scalar)
+        by_vector, by_scalar = nc.vector.tensor_copy, nc.scalar.copy
 
         ones = keep.tile([P, WARM_COLUMNS], F32)
         nc.gpsimd.memset(ones[:], 1.0)
@@ -117,9 +116,9 @@ def tile_windowattentionblock_pb_s_kernel(tc, attn_ctx, x, wo, bo, grad_out, out
             return (band * WINDOW + SHIFT) * WIDTH
 
         whole_bands = BANDS - 1
-        band_pairs = [load_pairs(image[band_start(0) : band_start(0) + BAND_PIXELS])]
         wo_pairs = load_pairs(wo_rows)
-        for band in range(1, whole_bands):
+        band_pairs = []
+        for band in range(whole_bands):
             band_pairs.append(load_pairs(image[band_start(band) : band_start(band) + BAND_PIXELS]))
         last_strips = []
         for h in range(STRIPS):
@@ -154,22 +153,22 @@ def tile_windowattentionblock_pb_s_kernel(tc, attn_ctx, x, wo, bo, grad_out, out
                 )
             return bank
 
-        def transpose_pairs(pair, column_order):
+        def transpose_pairs(pair, column_order, copies):
             grouped = bands.tile([P, PAIR * P * PACK], BF16, align_bytes=64, name="grouped")
             words = grouped[:].bitcast(F32).rearrange("p (e m half) -> p e m half", e=PAIR, half=HALVES)
             for e in range(PAIR):
                 bank = transpose_rows(pair[:, e, :], column_order)
-                copy_out[e % 2](out=words[:, e], in_=bank.rearrange("p half m -> p m half"))
+                copies[e](out=words[:, e], in_=bank.rearrange("p half m -> p m half"))
             return grouped
 
-        def transpose_strips(strips):
+        def transpose_strips(strips, copies):
             grouped = bands.tile([P, PAIR * P * PACK], BF16, align_bytes=64, name="grouped")
             words = grouped[:].bitcast(F32).rearrange(
                 "p (g h q half) -> p h g q half", g=PAIR * WINDOWS, h=STRIPS, half=HALVES
             )
             for h in range(STRIPS):
                 bank = transpose_rows(strips[h][:], strip_order[:])
-                copy_out[h % 2](
+                copies[h](
                     out=words[:, h],
                     in_=bank.rearrange("p half (g q) -> p g q half", g=PAIR * WINDOWS),
                 )
@@ -188,22 +187,7 @@ def tile_windowattentionblock_pb_s_kernel(tc, attn_ctx, x, wo, bo, grad_out, out
             nc.vector.quantize_mx(out=codes[:].bitcast(E5M2_X4), scales=scales[:], in_=grouped[:])
             band_codes.append((codes, scales))
 
-        band_codes = []
-        grouped_0 = transpose_pairs(band_pairs[0], pair_order[:])
-        keep_busy(ones[:, 0:P])
-        grouped_wo = transpose_pairs(wo_pairs, identity[:])
-        keep_busy(ones[:, 0:P])
-        quantise_band(grouped_0)
-        grouped_1 = transpose_pairs(band_pairs[1], pair_order[:])
-        keep_busy(ones[:, 0:P])
-        quantise_wo(grouped_wo)
-        grouped_2 = transpose_pairs(band_pairs[2], pair_order[:])
-        quantise_band(grouped_1)
-        grouped_3 = transpose_strips(last_strips)
-        quantise_band(grouped_2)
-        quantise_band(grouped_3)
-
-        for band in range(BANDS):
+        def multiply_band(band, copies):
             codes, scales = band_codes[band]
             rows = out_rows[band * BAND_PIXELS : (band + 1) * BAND_PIXELS].rearrange(
                 "(m e) f -> m e f", e=PAIR
@@ -220,8 +204,27 @@ def tile_windowattentionblock_pb_s_kernel(tc, attn_ctx, x, wo, bo, grad_out, out
                     stop=True,
                 )
                 result = results.tile([P, FEATURES], F32, name="result")
-                copy_out[(e + 1) % 2](
+                copies[e](
                     out=result[:].rearrange("p (m2 e2) -> p m2 e2", e2=PAIR),
                     in_=sums[:, 0:FEATURES].rearrange("p (e2 m2) -> p m2 e2", e2=PAIR),
                 )
-                store_queue[(e + 1) % 2].dma_start(out=rows[:, e, :], in_=result[:])
+                nc.sync.dma_start(out=rows[:, e, :], in_=result[:])
+
+        band_codes = []
+        grouped_wo = transpose_pairs(wo_pairs, identity[:], (by_vector, by_scalar))
+        keep_busy(ones[:, 0:P])
+        grouped_0 = transpose_pairs(band_pairs[0], pair_order[:], (by_vector, by_scalar))
+        keep_busy(ones[:, 0:P])
+        quantise_wo(grouped_wo)
+        quantise_band(grouped_0)
+        grouped_1 = transpose_pairs(band_pairs[1], pair_order[:], (by_scalar, by_vector))
+        keep_busy(ones[:, 0:P])
+        grouped_2 = transpose_pairs(band_pairs[2], pair_order[:], (by_scalar, by_scalar))
+        quantise_band(grouped_1)
+        multiply_band(0, (by_vector, by_scalar))
+        quantise_band(grouped_2)
+        grouped_3 = transpose_strips(last_strips, (by_vector, by_scalar))
+        quantise_band(grouped_3)
+        multiply_band(1, (by_scalar, by_scalar))
+        multiply_band(2, (by_vector, by_scalar))
+        multiply_band(3, (by_vector, by_scalar))

@@ -107,30 +107,38 @@ def tile_windowattentionblock_pb_s_kernel(tc, attn_ctx, x, wo, bo, grad_out, out
 
         keep_busy(ones[:, 0:P])
 
-        def load_pairs(rows):
-            pair = bands.tile([P, PAIR, CHANNELS], BF16, name="pair")
-            nc.sync.dma_start(out=pair[:], in_=rows.rearrange("(p e) c -> p e c", e=PAIR))
-            return pair
+        raw = {}
+        grouped = {}
+        quantised = {}
+        open_banks = {}
+
+        def load_pair(unit, rows):
+            raw[unit] = keep.tile([P, PAIR, CHANNELS], BF16, name="pair" + unit)
+            nc.sync.dma_start(out=raw[unit][:], in_=rows.rearrange("(p e) c -> p e c", e=PAIR))
 
         def band_start(band):
             return (band * WINDOW + SHIFT) * WIDTH
 
-        whole_bands = BANDS - 1
-        wo_pairs = load_pairs(wo_rows)
-        band_pairs = []
-        for band in range(whole_bands):
-            band_pairs.append(load_pairs(image[band_start(band) : band_start(band) + BAND_PIXELS]))
-        last_strips = []
-        for h in range(STRIPS):
-            first = (band_start(whole_bands) + h * P) % (HEIGHT * WIDTH)
-            strip = keep.tile([P, CHANNELS], BF16, name="strip%d" % h)
-            nc.sync.dma_start(out=strip[:], in_=image[first : first + P])
-            last_strips.append(strip)
+        def band_rows(band):
+            return image[band_start(band) : band_start(band) + BAND_PIXELS]
+
+        def load_strips():
+            raw["3"] = keep.tile([P, STRIPS, CHANNELS], BF16, name="strips")
+            for h in range(STRIPS):
+                first = (band_start(BANDS - 1) + h * P) % (HEIGHT * WIDTH)
+                nc.sync.dma_start(out=raw["3"][:, h, :], in_=image[first : first + P])
+
+        load_pair("w", wo_rows)
+        load_pair("0", band_rows(0))
+        load_pair("1", band_rows(1))
+        load_strips()
+        load_pair("2", band_rows(2))
 
         wo_codes = keep.tile([P, MOVING_COLUMNS], U32, align_bytes=64)
         wo_scales = keep.tile([P, MOVING_COLUMNS], U8, align_bytes=64)
         nc.vector.memset(wo_codes[:, FEATURES:MOVING_COLUMNS].bitcast(I32), 0)
         nc.vector.memset(wo_scales[:, FEATURES:MOVING_COLUMNS].bitcast(I32), 0)
+        quantised["w"] = (wo_codes, wo_scales, E4M3_X4)
 
         identity = keep.tile([P, P], F32)
         make_identity(nc, identity[:])
@@ -140,91 +148,116 @@ def tile_windowattentionblock_pb_s_kernel(tc, attn_ctx, x, wo, bo, grad_out, out
         keep_busy(pair_order[:])
         strip_order = keep.tile([P, P], F32)
         make_strip_order(nc, strip_order[:], identity[:])
+        orders = {"w": identity, "0": pair_order, "1": pair_order, "2": pair_order, "3": strip_order}
+        for unit in "w0123":
+            grouped[unit] = keep.tile([P, PAIR * P * PACK], BF16, align_bytes=64, name="grouped" + unit)
+        for unit in "0123":
+            codes = keep.tile([P, PAIR * P], U32, align_bytes=64, name="codes" + unit)
+            scales = keep.tile([P, PAIR * P], U8, align_bytes=64, name="scales" + unit)
+            quantised[unit] = (codes, scales, E5M2_X4)
 
-        def transpose_rows(rows, column_order):
-            whole_bank = banks.tile([P, MOVING_COLUMNS], F32, name="bank")
-            bank = whole_bank[:, 0 : HALVES * P].rearrange("p (half j) -> p half j", half=HALVES)
-            words = rows.bitcast(F32)
+        def transpose_bank(unit, e):
+            bank = banks.tile([P, MOVING_COLUMNS], F32, name="bank")
+            words = raw[unit][:, e, :].bitcast(F32)
             for half in range(HALVES):
                 nc.tensor.transpose(
-                    out=bank[:, half, :],
+                    out=bank[:, half * P : (half + 1) * P],
                     in_=words[:, half * P : (half + 1) * P],
-                    identity=column_order,
+                    identity=orders[unit][:],
                 )
-            return bank
+            open_banks[(unit, e)] = bank
 
-        def transpose_pairs(pair, column_order, copies):
-            grouped = bands.tile([P, PAIR * P * PACK], BF16, align_bytes=64, name="grouped")
-            words = grouped[:].bitcast(F32).rearrange("p (e m half) -> p e m half", e=PAIR, half=HALVES)
-            for e in range(PAIR):
-                bank = transpose_rows(pair[:, e, :], column_order)
-                copies[e](out=words[:, e], in_=bank.rearrange("p half m -> p m half"))
-            return grouped
-
-        def transpose_strips(strips, copies):
-            grouped = bands.tile([P, PAIR * P * PACK], BF16, align_bytes=64, name="grouped")
-            words = grouped[:].bitcast(F32).rearrange(
-                "p (g h q half) -> p h g q half", g=PAIR * WINDOWS, h=STRIPS, half=HALVES
-            )
-            for h in range(STRIPS):
-                bank = transpose_rows(strips[h][:], strip_order[:])
-                copies[h](
-                    out=words[:, h],
-                    in_=bank.rearrange("p half (g q) -> p g q half", g=PAIR * WINDOWS),
+        def copy_bank(unit, e, copy):
+            bank = open_banks[(unit, e)][:, 0 : HALVES * P]
+            words = grouped[unit][:].bitcast(F32)
+            if unit == "3":
+                copy(
+                    out=words.rearrange("p (g h q half) -> p h g q half", g=PAIR * WINDOWS, h=STRIPS, half=HALVES)[:, e],
+                    in_=bank.rearrange("p (half g q) -> p g q half", half=HALVES, g=PAIR * WINDOWS),
                 )
-            return grouped
+            else:
+                copy(
+                    out=words.rearrange("p (e m half) -> p e m half", e=PAIR, half=HALVES)[:, e],
+                    in_=bank.rearrange("p (half m) -> p m half", half=HALVES),
+                )
 
-        def quantise_wo(grouped):
+        def quantise(unit, e):
+            codes, scales, form = quantised[unit]
+            columns = slice(0, PAIR * P) if e is None else slice(e * P, (e + 1) * P)
             nc.vector.quantize_mx(
-                out=wo_codes[:, 0:FEATURES].bitcast(E4M3_X4),
-                scales=wo_scales[:, 0:FEATURES],
-                in_=grouped[:],
+                out=codes[:, columns].bitcast(form),
+                scales=scales[:, columns],
+                in_=grouped[unit][:, columns.start * PACK : columns.stop * PACK],
             )
 
-        def quantise_band(grouped):
-            codes = bands.tile([P, PAIR * P], U32, align_bytes=64, name="codes")
-            scales = bands.tile([P, PAIR * P], U8, align_bytes=64, name="scales")
-            nc.vector.quantize_mx(out=codes[:].bitcast(E5M2_X4), scales=scales[:], in_=grouped[:])
-            band_codes.append((codes, scales))
-
-        def multiply_band(band, copies):
-            codes, scales = band_codes[band]
-            rows = out_rows[band * BAND_PIXELS : (band + 1) * BAND_PIXELS].rearrange(
-                "(m e) f -> m e f", e=PAIR
+        def multiply(unit, e):
+            codes, scales, form = quantised[unit]
+            sums = banks.tile([P, MOVING_COLUMNS], F32, name="bank")
+            nc.tensor.matmul_mx(
+                out=sums[:],
+                lhsT=codes[:, e * P : (e + 1) * P].bitcast(form),
+                lhsT_scale=scales[:, e * P : (e + 1) * P],
+                rhs=wo_codes[:].bitcast(E4M3_X4),
+                rhs_scale=wo_scales[:],
+                start=True,
+                stop=True,
             )
-            for e in range(PAIR):
-                sums = banks.tile([P, MOVING_COLUMNS], F32, name="bank")
-                nc.tensor.matmul_mx(
-                    out=sums[:],
-                    lhsT=codes[:, e * P : (e + 1) * P].bitcast(E5M2_X4),
-                    lhsT_scale=scales[:, e * P : (e + 1) * P],
-                    rhs=wo_codes[:].bitcast(E4M3_X4),
-                    rhs_scale=wo_scales[:],
-                    start=True,
-                    stop=True,
-                )
-                result = results.tile([P, FEATURES], F32, name="result")
-                copies[e](
-                    out=result[:].rearrange("p (m2 e2) -> p m2 e2", e2=PAIR),
-                    in_=sums[:, 0:FEATURES].rearrange("p (e2 m2) -> p m2 e2", e2=PAIR),
-                )
-                nc.sync.dma_start(out=rows[:, e, :], in_=result[:])
+            open_banks[(unit, PAIR + e)] = sums
 
-        band_codes = []
-        grouped_wo = transpose_pairs(wo_pairs, identity[:], (by_vector, by_scalar))
+        def copy_product(unit, e, copy, queue):
+            band = int(unit)
+            rows = out_rows[band * BAND_PIXELS : (band + 1) * BAND_PIXELS].rearrange("(m e) f -> m e f", e=PAIR)
+            result = results.tile([P, FEATURES], F32, name="result")
+            copy(
+                out=result[:].rearrange("p (m2 e2) -> p m2 e2", e2=PAIR),
+                in_=open_banks[(unit, PAIR + e)][:, 0:FEATURES].rearrange("p (e2 m2) -> p m2 e2", e2=PAIR),
+            )
+            queue.dma_start(out=rows[:, e, :], in_=result[:])
+
+        transpose_bank("w", 0)
+        copy_bank("w", 0, by_vector)
+        transpose_bank("w", 1)
+        copy_bank("w", 1, by_scalar)
         keep_busy(ones[:, 0:P])
-        grouped_0 = transpose_pairs(band_pairs[0], pair_order[:], (by_vector, by_scalar))
+        transpose_bank("0", 0)
+        copy_bank("0", 0, by_vector)
+        quantise("w", None)
+        quantise("0", 0)
+        transpose_bank("0", 1)
+        copy_bank("0", 1, by_scalar)
+        quantise("0", 1)
         keep_busy(ones[:, 0:P])
-        quantise_wo(grouped_wo)
-        quantise_band(grouped_0)
-        grouped_1 = transpose_pairs(band_pairs[1], pair_order[:], (by_scalar, by_vector))
+        transpose_bank("1", 0)
+        copy_bank("1", 0, by_vector)
+        transpose_bank("1", 1)
+        copy_bank("1", 1, by_scalar)
         keep_busy(ones[:, 0:P])
-        grouped_2 = transpose_pairs(band_pairs[2], pair_order[:], (by_scalar, by_scalar))
-        quantise_band(grouped_1)
-        multiply_band(0, (by_vector, by_scalar))
-        quantise_band(grouped_2)
-        grouped_3 = transpose_strips(last_strips, (by_vector, by_scalar))
-        quantise_band(grouped_3)
-        multiply_band(1, (by_scalar, by_scalar))
-        multiply_band(2, (by_vector, by_scalar))
-        multiply_band(3, (by_vector, by_scalar))
+        transpose_bank("3", 0)
+        copy_bank("3", 0, by_vector)
+        quantise("1", 0)
+        quantise("1", 1)
+        transpose_bank("3", 1)
+        copy_bank("3", 1, by_scalar)
+        quantise("3", None)
+        multiply("0", 0)
+        copy_product("0", 0, by_scalar, nc.sync)
+        multiply("0", 1)
+        copy_product("0", 1, by_scalar, nc.sync)
+        transpose_bank("2", 0)
+        copy_bank("2", 0, by_vector)
+        quantise("2", 0)
+        transpose_bank("2", 1)
+        copy_bank("2", 1, by_scalar)
+        quantise("2", 1)
+        multiply("1", 0)
+        copy_product("1", 0, by_scalar, nc.sync)
+        multiply("1", 1)
+        copy_product("1", 1, by_vector, nc.sync)
+        multiply("3", 0)
+        copy_product("3", 0, by_scalar, nc.sync)
+        multiply("3", 1)
+        copy_product("3", 1, by_vector, nc.sync)
+        multiply("2", 0)
+        copy_product("2", 0, by_scalar, nc.sync)
+        multiply("2", 1)
+        copy_product("2", 1, by_vector, nc.sync)

@@ -215,49 +215,48 @@ def tile_windowattentionblock_pb_s_kernel(tc, attn_ctx, x, wo, bo, grad_out, out
             queue.dma_start(out=rows[:, e, :], in_=result[:])
 
         transpose_bank("w", 0)
-        copy_bank("w", 0, by_vector)
+        copy_bank("w", 0, by_scalar)
         transpose_bank("w", 1)
         copy_bank("w", 1, by_scalar)
+        quantise("w", None)
         keep_busy(ones[:, 0:P])
         transpose_bank("0", 0)
-        copy_bank("0", 0, by_vector)
-        quantise("w", None)
+        copy_bank("0", 0, by_scalar)
         quantise("0", 0)
         transpose_bank("0", 1)
         copy_bank("0", 1, by_scalar)
         quantise("0", 1)
         keep_busy(ones[:, 0:P])
         transpose_bank("1", 0)
-        copy_bank("1", 0, by_vector)
+        copy_bank("1", 0, by_scalar)
+        quantise("1", 0)
         transpose_bank("1", 1)
         copy_bank("1", 1, by_scalar)
-        keep_busy(ones[:, 0:P])
-        transpose_bank("3", 0)
-        copy_bank("3", 0, by_vector)
-        quantise("1", 0)
         quantise("1", 1)
+        transpose_bank("3", 0)
+        copy_bank("3", 0, by_scalar)
         transpose_bank("3", 1)
         copy_bank("3", 1, by_scalar)
-        quantise("3", None)
         multiply("0", 0)
-        copy_product("0", 0, by_scalar, nc.sync)
+        copy_product("0", 0, by_vector, nc.sync)
+        quantise("3", None)
         multiply("0", 1)
         copy_product("0", 1, by_scalar, nc.sync)
         transpose_bank("2", 0)
-        copy_bank("2", 0, by_vector)
-        quantise("2", 0)
+        copy_bank("2", 0, by_scalar)
         transpose_bank("2", 1)
-        copy_bank("2", 1, by_scalar)
+        copy_bank("2", 1, by_vector)
+        quantise("2", 0)
         quantise("2", 1)
         multiply("1", 0)
         copy_product("1", 0, by_scalar, nc.sync)
         multiply("1", 1)
-        copy_product("1", 1, by_vector, nc.sync)
+        copy_product("1", 1, by_scalar, nc.sync)
         multiply("3", 0)
-        copy_product("3", 0, by_scalar, nc.sync)
+        copy_product("3", 0, by_vector, nc.sync)
         multiply("3", 1)
-        copy_product("3", 1, by_vector, nc.sync)
+        copy_product("3", 1, by_scalar, nc.sync)
         multiply("2", 0)
-        copy_product("2", 0, by_scalar, nc.sync)
+        copy_product("2", 0, by_vector, nc.sync)
         multiply("2", 1)
-        copy_product("2", 1, by_vector, nc.sync)
+        copy_product("2", 1, by_scalar, nc.sync)

@@ -132,7 +132,11 @@ def tile_windowattentionblock_pb_s_kernel(tc, attn_ctx, x, wo, bo, grad_out, out
         load_pair("0", band_rows(0))
         load_pair("1", band_rows(1))
         load_strips()
-        load_pair("2", band_rows(2))
+        raw["2"] = keep.tile([P, PAIR, CHANNELS], BF16, name="pair2")
+        for e in range(PAIR):
+            nc.sync.dma_start(
+                out=raw["2"][:, e, :], in_=band_rows(2).rearrange("(p e) c -> p e c", e=PAIR)[:, e, :]
+            )
 
         wo_codes = keep.tile([P, MOVING_COLUMNS], U32, align_bytes=64)
         wo_scales = keep.tile([P, MOVING_COLUMNS], U8, align_bytes=64)
@@ -237,9 +241,9 @@ def tile_windowattentionblock_pb_s_kernel(tc, attn_ctx, x, wo, bo, grad_out, out
         copy_bank("3", 0, by_scalar)
         transpose_bank("3", 1)
         copy_bank("3", 1, by_scalar)
-        multiply("0", 0)
-        copy_product("0", 0, by_vector, nc.sync)
         quantise("3", None)
+        multiply("0", 0)
+        copy_product("0", 0, by_scalar, nc.sync)
         multiply("0", 1)
         copy_product("0", 1, by_scalar, nc.sync)
         transpose_bank("2", 0)
@@ -253,10 +257,10 @@ def tile_windowattentionblock_pb_s_kernel(tc, attn_ctx, x, wo, bo, grad_out, out
         multiply("1", 1)
         copy_product("1", 1, by_scalar, nc.sync)
         multiply("3", 0)
-        copy_product("3", 0, by_vector, nc.sync)
+        copy_product("3", 0, by_scalar, nc.sync)
         multiply("3", 1)
-        copy_product("3", 1, by_scalar, nc.sync)
+        copy_product("3", 1, by_vector, nc.sync)
         multiply("2", 0)
-        copy_product("2", 0, by_vector, nc.sync)
+        copy_product("2", 0, by_scalar, nc.sync)
         multiply("2", 1)
-        copy_product("2", 1, by_scalar, nc.sync)
+        copy_product("2", 1, by_vector, nc.sync)

from contextlib import ExitStack

import concourse.mybir as mybir
from concourse.masks import make_identity

BF16 = mybir.dt.bfloat16
F32 = mybir.dt.float32
I32 = mybir.dt.int32
U32 = mybir.dt.uint32
U8 = mybir.dt.uint8
E5M2_X4 = mybir.dt.float8_e5m2_x4
E4M3_X4 = mybir.dt.float8_e4m3fn_x4

P = 128
HEIGHT = 32
WIDTH = 32
CHANNELS = 512
FEATURES = 256
WINDOW = 8
SHIFT = 4
BANDS = HEIGHT // WINDOW
WINDOWS = WIDTH // WINDOW
BAND_PIXELS = WINDOW * WIDTH
PAIR = BAND_PIXELS // P
STRIP_ROWS = P // WIDTH
STRIPS = BAND_PIXELS // P
HALVES = 2
PACK = 4
MOVING_COLUMNS = 512
PSUM_BANKS = 8
WARM_COLUMNS = 136

FLOPS = 2 * HEIGHT * WIDTH * FEATURES * CHANNELS
BYTES = 2 * HEIGHT * WIDTH * CHANNELS + 2 * FEATURES * CHANNELS + 4 * HEIGHT * WIDTH * FEATURES


def make_pair_order(nc, pair_order, identity):
    pairs = WIDTH // PAIR
    in_window = WINDOW // PAIR
    shift = SHIFT // PAIR
    from_image = identity.rearrange("p (row pair) -> p row pair", pair=pairs)
    to_window = pair_order.rearrange("p (win row pair) -> p win row pair", win=WINDOWS, pair=in_window)
    last = WINDOWS - 1
    nc.vector.tensor_copy(
        out=to_window[:, 0:last],
        in_=from_image[:, :, shift : shift + last * in_window].rearrange(
            "p row (win pair) -> p win row pair", pair=in_window
        ),
    )
    nc.vector.tensor_copy(
        out=to_window[:, last, :, 0 : in_window - shift],
        in_=from_image[:, :, shift + last * in_window : pairs],
    )
    nc.vector.tensor_copy(
        out=to_window[:, last, :, in_window - shift : in_window], in_=from_image[:, :, 0:shift]
    )


def make_strip_order(nc, strip_order, identity):
    in_window = WINDOW // PAIR
    from_image = identity.rearrange("p (row col) -> p row col", col=WIDTH)
    to_window = strip_order.rearrange(
        "p (e win row pair) -> p e win row pair", e=PAIR, win=WINDOWS, pair=in_window
    )
    last = WINDOWS - 1
    wrap = SHIFT + last * WINDOW
    for e in range(PAIR):
        nc.vector.tensor_copy(
            out=to_window[:, e, 0:last],
            in_=from_image[:, :, SHIFT + e : wrap + e : PAIR].rearrange(
                "p row (win pair) -> p win row pair", pair=in_window
            ),
        )
        nc.vector.tensor_copy(
            out=to_window[:, e, last, :, 0 : (WIDTH - wrap) // PAIR],
            in_=from_image[:, :, wrap + e : WIDTH : PAIR],
        )
        nc.vector.tensor_copy(
            out=to_window[:, e, last, :, (WIDTH - wrap) // PAIR : in_window],
            in_=from_image[:, :, e : SHIFT : PAIR],
        )


def tile_windowattentionblock_pb_s_kernel(tc, attn_ctx, x, wo, bo, grad_out, out):
    nc = tc.nc
    image = grad_out.rearrange("b i j c -> (b i j) c")
    wo_rows = wo.rearrange("h d c -> (h d) c")
    out_rows = out.rearrange("n t h d -> (n t) (h d)")

    with ExitStack() as stack:
        keep = stack.enter_context(tc.tile_pool(name="keep", bufs=1))
        bands = stack.enter_context(tc.tile_pool(name="bands", bufs=BANDS + 1))
        results = stack.enter_context(tc.tile_pool(name="results", bufs=BANDS * PAIR))
        banks = stack.enter_context(tc.psum_pool(name="banks", bufs=PSUM_BANKS))
        stack.enter_context(tc.manual_schedule())

        by_vector, by_scalar = nc.vector.tensor_copy, nc.scalar.copy

        ones = keep.tile([P, WARM_COLUMNS], F32)
        nc.gpsimd.memset(ones[:], 1.0)

        def keep_busy(stationary):
            unread = banks.tile([P, MOVING_COLUMNS], F32, name="bank")
            nc.tensor.matmul(
                out=unread[:, 0:WARM_COLUMNS], lhsT=stationary, rhs=ones[:], start=True, stop=True
            )

        keep_busy(ones[:, 0:P])

        raw = {}
        grouped = {}
        quantised = {}
        open_banks = {}

        def load_pair(unit, rows):
            raw[unit] = keep.tile([P, PAIR, CHANNELS], BF16, name="pair" + unit)
            nc.sync.dma_start(out=raw[unit][:], in_=rows.rearrange("(p e) c -> p e c", e=PAIR))

        def band_start(band):
            return (band * WINDOW + SHIFT) * WIDTH

        def band_rows(band):
            return image[band_start(band) : band_start(band) + BAND_PIXELS]

        def load_strips():
            raw["3"] = keep.tile([P, STRIPS, CHANNELS], BF16, name="strips")
            for h in range(STRIPS):
                first = (band_start(BANDS - 1) + h * P) % (HEIGHT * WIDTH)
                nc.sync.dma_start(out=raw["3"][:, h, :], in_=image[first : first + P])

        load_pair("w", wo_rows)
        load_pair("0", band_rows(0))
        load_pair("1", band_rows(1))
        load_strips()
        raw["2"] = keep.tile([P, PAIR, CHANNELS], BF16, name="pair2")
        for e in range(PAIR):
            nc.sync.dma_start(
                out=raw["2"][:, e, :], in_=band_rows(2).rearrange("(p e) c -> p e c", e=PAIR)[:, e, :]
            )

        wo_codes = keep.tile([P, MOVING_COLUMNS], U32, align_bytes=64)
        wo_scales = keep.tile([P, MOVING_COLUMNS], U8, align_bytes=64)
        nc.vector.memset(wo_codes[:, FEATURES:MOVING_COLUMNS].bitcast(I32), 0)
        nc.vector.memset(wo_scales[:, FEATURES:MOVING_COLUMNS].bitcast(I32), 0)
        quantised["w"] = (wo_codes, wo_scales, E4M3_X4)

        identity = keep.tile([P, P], F32)
        make_identity(nc, identity[:])
        keep_busy(identity[:])
        pair_order = keep.tile([P, P], F32)
        make_pair_order(nc, pair_order[:], identity[:])
        keep_busy(pair_order[:])
        strip_order = keep.tile([P, P], F32)
        make_strip_order(nc, strip_order[:], identity[:])
        orders = {"w": identity, "0": pair_order, "1": pair_order, "2": pair_order, "3": strip_order}
        for unit in "w0123":
            grouped[unit] = keep.tile([P, PAIR * P * PACK], BF16, align_bytes=64, name="grouped" + unit)
        for unit in "0123":
            codes = keep.tile([P, PAIR * P], U32, align_bytes=64, name="codes" + unit)
            scales = keep.tile([P, PAIR * P], U8, align_bytes=64, name="scales" + unit)
            quantised[unit] = (codes, scales, E5M2_X4)

        def transpose_bank(unit, e):
            bank = banks.tile([P, MOVING_COLUMNS], F32, name="bank")
            words = raw[unit][:, e, :].bitcast(F32)
            for half in range(HALVES):
                nc.tensor.transpose(
                    out=bank[:, half * P : (half + 1) * P],
                    in_=words[:, half * P : (half + 1) * P],
                    identity=orders[unit][:],
                )
            open_banks[(unit, e)] = bank

        def copy_bank(unit, e, copy):
            bank = open_banks[(unit, e)][:, 0 : HALVES * P]
            words = grouped[unit][:].bitcast(F32)
            if unit == "3":
                copy(
                    out=words.rearrange("p (g h q half) -> p h g q half", g=PAIR * WINDOWS, h=STRIPS, half=HALVES)[:, e],
                    in_=bank.rearrange("p (half g q) -> p g q half", half=HALVES, g=PAIR * WINDOWS),
                )
            else:
                copy(
                    out=words.rearrange("p (e m half) -> p e m half", e=PAIR, half=HALVES)[:, e],
                    in_=bank.rearrange("p (half m) -> p m half", half=HALVES),
                )

        def quantise(unit, e):
            codes, scales, form = quantised[unit]
            columns = slice(0, PAIR * P) if e is None else slice(e * P, (e + 1) * P)
            nc.vector.quantize_mx(
                out=codes[:, columns].bitcast(form),
                scales=scales[:, columns],
                in_=grouped[unit][:, columns.start * PACK : columns.stop * PACK],
            )

        def multiply(unit, e):
            codes, scales, form = quantised[unit]
            sums = banks.tile([P, MOVING_COLUMNS], F32, name="bank")
            nc.tensor.matmul_mx(
                out=sums[:],
                lhsT=codes[:, e * P : (e + 1) * P].bitcast(form),
                lhsT_scale=scales[:, e * P : (e + 1) * P],
                rhs=wo_codes[:].bitcast(E4M3_X4),
                rhs_scale=wo_scales[:],
                start=True,
                stop=True,
            )
            open_banks[(unit, PAIR + e)] = sums

        def copy_product(unit, e, copy, queue):
            band = int(unit)
            rows = out_rows[band * BAND_PIXELS : (band + 1) * BAND_PIXELS].rearrange("(m e) f -> m e f", e=PAIR)
            result = results.tile([P, FEATURES], F32, name="result")
            copy(
                out=result[:].rearrange("p (m2 e2) -> p m2 e2", e2=PAIR),
                in_=open_banks[(unit, PAIR + e)][:, 0:FEATURES].rearrange("p (e2 m2) -> p m2 e2", e2=PAIR),
            )
            queue.dma_start(out=rows[:, e, :], in_=result[:])

        transpose_bank("w", 0)
        copy_bank("w", 0, by_scalar)
        transpose_bank("w", 1)
        copy_bank("w", 1, by_scalar)
        quantise("w", None)
        keep_busy(ones[:, 0:P])
        transpose_bank("0", 0)
        copy_bank("0", 0, by_scalar)
        quantise("0", 0)
        transpose_bank("0", 1)
        copy_bank("0", 1, by_scalar)
        quantise("0", 1)
        keep_busy(ones[:, 0:P])
        transpose_bank("1", 0)
        copy_bank("1", 0, by_scalar)
        quantise("1", 0)
        transpose_bank("1", 1)
        copy_bank("1", 1, by_scalar)
        quantise("1", 1)
        transpose_bank("3", 0)
        copy_bank("3", 0, by_scalar)
        transpose_bank("3", 1)
        copy_bank("3", 1, by_scalar)
        quantise("3", None)
        multiply("0", 0)
        copy_product("0", 0, by_scalar, nc.sync)
        multiply("0", 1)
        copy_product("0", 1, by_scalar, nc.sync)
        transpose_bank("2", 0)
        copy_bank("2", 0, by_scalar)
        transpose_bank("2", 1)
        copy_bank("2", 1, by_vector)
        quantise("2", 0)
        quantise("2", 1)
        multiply("1", 0)
        copy_product("1", 0, by_scalar, nc.sync)
        multiply("1", 1)
        copy_product("1", 1, by_scalar, nc.sync)
        multiply("3", 0)
        copy_product("3", 0, by_scalar, nc.sync)
        multiply("3", 1)
        copy_product("3", 1, by_vector, nc.sync)
        multiply("2", 0)
        copy_product("2", 0, by_scalar, nc.sync)
        multiply("2", 1)
        copy_product("2", 1, by_vector, nc.sync)
